import numpy as np
import ml_dtypes


def mxq(x, axis, fmt="e4m3"):
    dtype, down = {"e4m3": (ml_dtypes.float8_e4m3fn, 7), "e5m2": (ml_dtypes.float8_e5m2, 14)}[fmt]
    v = np.moveaxis(np.asarray(x, np.float32).astype(ml_dtypes.bfloat16).astype(np.float64), axis, -1)
    blocks = v.reshape(v.shape[:-1] + (-1, 32))
    amax = np.abs(blocks).max(-1, keepdims=True)
    byte = np.maximum(np.where(amax > 0, np.frexp(amax)[1] - 1 + 127, 0) - down, 1)
    scale = np.exp2(byte - 127.0)
    codes = (blocks / scale).astype(np.float32).astype(dtype).astype(np.float64)
    return np.moveaxis((codes * scale).reshape(v.shape), -1, axis)


WIDE = False


def mx_kscale(k):
    if not WIDE:
        return np.ones(k)
    levels = np.array([10, -10, 5, -5, 0])
    a = np.random.permutation(np.resize(levels, k // 512 * 4)).reshape(k // 512, 4)
    idx = np.arange(k)
    return np.exp2(a[idx // 512, idx % 128 // 32])


BF16 = ml_dtypes.bfloat16


def bf(x):
    return np.asarray(x, np.float32).astype(BF16)


def f64(x):
    return np.asarray(x).astype(np.float64)


B, T, D, F = 4, 128, 1024, 1024
K2, K3, K4 = 2, 3, 4
EPS = 1e-12


def conv_branch(xq, w, b):
    kw = w.shape[1]
    n = xq.shape[1] - kw + 1
    wq = mxq(f64(w), 2, "e4m3")
    out = sum((xq[:, k:k + n, :] @ wq[:, k, :].T) for k in range(kw))
    return np.maximum(out + f64(b), 0.0)


def l2norm(x, axis):
    n = np.sqrt(np.sum(x * x, axis=axis, keepdims=True))
    return x / np.maximum(n, EPS)


def setup_inputs():
    s = mx_kscale(D)
    return {"words_emb": bf(np.random.standard_normal((B, T, D)) * s),
            "W2": bf(np.random.standard_normal((F, K2, D)) / np.sqrt(K2 * D) / s), "b2": bf(np.random.standard_normal(F) * 0.3),
            "W3": bf(np.random.standard_normal((F, K3, D)) / np.sqrt(K3 * D) / s), "b3": bf(np.random.standard_normal(F) * 0.3),
            "W4": bf(np.random.standard_normal((F, K4, D)) / np.sqrt(K4 * D) / s), "b4": bf(np.random.standard_normal(F) * 0.3)}


def reference(words_emb, W2, b2, W3, b3, W4, b4):
    xq = mxq(f64(words_emb), 2, "e4m3")
    a = conv_branch(xq, W2, b2)
    b_ = conv_branch(xq, W3, b3)
    c = conv_branch(xq, W4, b4)
    seq = T - K4 + 1
    main = np.maximum(np.maximum(a[:, :seq], b_[:, :seq]), c[:, :seq])
    pen = np.maximum(a[:, seq], b_[:, seq])[:, None]
    last = a[:, seq + 1][:, None]
    code = np.concatenate([main, pen, last], axis=1)
    code = l2norm(code, 2)
    return code.transpose(0, 2, 1)

@@ -1,0 +1,232 @@
+from contextlib import ExitStack
+
+import concourse.mybir as mybir
+from concourse.masks import make_identity
+
+F32 = mybir.dt.float32
+BF16 = mybir.dt.bfloat16
+U32 = mybir.dt.uint32
+U8 = mybir.dt.uint8
+FP8X4 = mybir.dt.float8_e4m3fn_x4
+ACT = mybir.ActivationFunctionType
+ALU = mybir.AluOpType
+
+P = 128
+B = 4
+T = 128
+D = 1024
+F = 1024
+NI = F // P
+WIDTHS = (2, 3, 4)
+R = 4
+NPL = R + 3
+FLOPS = 2 * B * (127 * 2 + 126 * 3 + 125 * 4) * D * F
+MANUAL = True
+COPY_ENG = {2: "SS", 3: "VSV", 4: "SSVS"}
+
+
+def tile_textheading_pa_kernel(tc, words_emb, W2, b2, W3, b3, W4, b4, out):
+    nc = tc.nc
+    Wd = {2: W2, 3: W3, 4: W4}
+    bd = {2: b2, 3: b3, 4: b4}
+    with ExitStack() as ctx:
+        if MANUAL:
+            ctx.enter_context(tc.manual_schedule())
+        const = ctx.enter_context(tc.tile_pool(name="const", bufs=1))
+        wpool = ctx.enter_context(tc.tile_pool(name="wraw", bufs=3))
+        gpool = ctx.enter_context(tc.tile_pool(name="grp", bufs=2))
+        cpool = ctx.enter_context(tc.tile_pool(name="codes", bufs=3))
+        epool = ctx.enter_context(tc.tile_pool(name="epi", bufs=2))
+        tp = ctx.enter_context(tc.psum_pool(name="tp", bufs=5))
+        accp = ctx.enter_context(tc.psum_pool(name="acc", bufs=1))
+
+        ident = const.tile([P, P], F32, name="ident")
+        make_identity(nc, ident[:])
+        ones = const.tile([P, P], F32, name="ones")
+        nc.vector.memset(ones[:], 1.0)
+
+        braw = {}
+        for K in WIDTHS:
+            braw[K] = const.tile([P, NI], BF16, name="braw%d" % K)
+            nc.scalar.dma_start(out=braw[K][:], in_=bd[K].rearrange("(m i) -> m i", i=NI))
+        bias = const.tile([P, 3, NI], F32, name="bias")
+        warm = const.tile([P, 1], F32, name="warm")
+        nc.scalar.activation(out=warm[:], in_=ones[:, 0:1], func=ACT.Abs_reciprocal_sqrt)
+
+        x_sb = const.tile([P, B, D], BF16, name="x_sb")
+        for n in range(B):
+            nc.sync.dma_start(out=x_sb[:, n, :], in_=words_emb[n])
+        Wv = {}
+        for K in WIDTHS:
+            Wv[K] = Wd[K].rearrange("(m i) k d -> i m (k d)", i=NI)
+        wraw = {}
+
+        def load(i):
+            for K in WIDTHS:
+                wraw[(i, K)] = wpool.tile([P, K * D], BF16, name="w%d" % K, tag="w%d" % K)
+                nc.sync.dma_start(out=wraw[(i, K)][:], in_=Wv[K][i])
+
+        for i in range(3):
+            load(i)
+
+        def copy(eng, dst, src):
+            if eng == "V":
+                nc.vector.tensor_copy(out=dst, in_=src)
+            else:
+                nc.scalar.copy(out=dst, in_=src)
+
+        XC = NPL * B * 32
+        xg = const.tile([P, 2 * XC * 4], BF16, name="xg", align_bytes=64)
+        xg_w = xg[:].bitcast(F32).rearrange("p (g r n q u) -> p g r n q u", g=2, r=NPL, n=B, q=32, u=2)
+        xc = const.tile([P, 2, XC], U32, name="xc", align_bytes=64)
+        xs = const.tile([P, 2, XC], U8, name="xs", align_bytes=64)
+        for g in range(2):
+            nc.vector.memset(xg_w[:, g, R:NPL, :, 31:32, :], 0.0)
+        for n in range(B):
+            xb = tp.tile([P, 2, 2, P], F32, name="xb", tag="tp")
+            xw = x_sb[:, n, :].bitcast(F32)
+            for g in range(2):
+                for u in range(2):
+                    o = 256 * g + 128 * u
+                    nc.tensor.transpose(xb[:, g, u, :], xw[:, o:o + P], ident[:])
+            for g in range(2):
+                copy("VS"[n % 2], xg_w[:, g, 0:R, n, :, :], xb[:, g, :, :].rearrange("p u (q r) -> p r q u", r=R))
+        for g in range(2):
+            nc.vector.tensor_copy(out=xg_w[:, g, R:NPL, :, 0:31, :], in_=xg_w[:, g, 0:3, :, 1:32, :])
+
+        def quant_x(g, pl0, npl):
+            c0 = pl0 * P
+            w = npl * P
+            a = (g * XC + c0) * 4
+            nc.vector.quantize_mx(out=xc[:, g, c0:c0 + w].bitcast(FP8X4), scales=xs[:, g, c0:c0 + w],
+                                  in_=xg[:, a:a + 4 * w])
+
+        grp = {}
+        cod = {}
+
+        def transposes(i, K, engs):
+            gr = gpool.tile([P, K * 1024], BF16, name="g%d" % K, tag="g%d" % K, align_bytes=64)
+            grp[(i, K)] = gr
+            gr_w = gr[:].bitcast(F32).rearrange("p (k g f u) -> p k g f u", k=K, g=2, f=P, u=2)
+            ww = wraw[(i, K)][:].bitcast(F32)
+            for k in range(K):
+                bank = tp.tile([P, 2, 2, P], F32, name="bank", tag="tp")
+                for g in range(2):
+                    for u in range(2):
+                        o = 512 * k + 256 * g + 128 * u
+                        nc.tensor.transpose(bank[:, g, u, :], ww[:, o:o + P], ident[:])
+                copy(engs[k], gr_w[:, k], bank[:].rearrange("p g u f -> p g f u"))
+
+        def quantise(i, K):
+            cw = cpool.tile([P, K * 256], U32, name="c%d" % K, tag="c%d" % K, align_bytes=64)
+            sc = cpool.tile([P, K * 256], U8, name="s%d" % K, tag="s%d" % K, align_bytes=64)
+            cod[(i, K)] = (cw, sc)
+            gr = grp[(i, K)]
+            for (a, w) in {2: ((0, 2048),), 3: ((0, 2048), (2048, 1024)), 4: ((0, 4096),)}[K]:
+                nc.vector.quantize_mx(out=cw[:, a // 4:(a + w) // 4].bitcast(FP8X4),
+                                      scales=sc[:, a // 4:(a + w) // 4], in_=gr[:, a:a + w])
+
+        Tn = const.tile([P, NI, B, T], F32, name="Tn")
+        ssum = const.tile([P, B, T], F32, name="ssum")
+        rinv = const.tile([P, B, T], F32, name="rinv")
+        O = const.tile([P, B, NI * (T - 1)], F32, name="O")
+        accs = {}
+        tmp = {}
+        sqs = {}
+
+        def products(i, K):
+            acc = accp.tile([P, 512], F32, name="acc%d" % K, tag="acc%d" % K)
+            accs[(i, K)] = acc
+            cw, sc = cod[(i, K)]
+            for k in range(K):
+                for g in range(2):
+                    j = (2 * k + g) * P
+                    nc.tensor.matmul_mx(out=acc[:], lhsT=cw[:, j:j + P].bitcast(FP8X4), lhsT_scale=sc[:, j:j + P],
+                                        rhs=xc[:, g, P * k:P * k + 512].bitcast(FP8X4),
+                                        rhs_scale=xs[:, g, P * k:P * k + 512],
+                                        start=(k == 0 and g == 0), stop=(k == K - 1 and g == 1))
+
+        def relu(i, K):
+            if K == 2:
+                dst = Tn[:, i]
+            else:
+                tmp[(i, K)] = epool.tile([P, B, T], F32, name="t%d" % K, tag="t%d" % K)
+                dst = tmp[(i, K)][:]
+            nc.scalar.activation(out=dst.rearrange("p n (q r) -> p n q r", r=R),
+                                 in_=accs[(i, K)][:].rearrange("p (r n q) -> p n q r", r=R, n=B),
+                                 func=ACT.Relu, bias=bias[:, K - 2, i:i + 1])
+
+        def maxi(i, K):
+            v = T + 1 - K
+            nc.vector.tensor_tensor(out=Tn[:, i, :, 0:v], in0=Tn[:, i, :, 0:v], in1=tmp[(i, K)][:, :, 0:v], op=ALU.max)
+
+        def square(i):
+            if i == 0:
+                nc.scalar.activation(out=ssum[:], in_=Tn[:, i], func=ACT.Square)
+            else:
+                sqs[i] = epool.tile([P, B, T], F32, name="sq", tag="sq")
+                nc.scalar.activation(out=sqs[i][:], in_=Tn[:, i], func=ACT.Square)
+
+        def addsq(i):
+            if i > 0:
+                nc.vector.tensor_tensor(out=ssum[:], in0=ssum[:], in1=sqs[i][:], op=ALU.add)
+
+        def finish():
+            rb = tp.tile([P, 512], F32, name="rb", tag="tp")
+            nc.tensor.matmul(out=rb[:], lhsT=ones[:], rhs=ssum[:].rearrange("p n q -> p (n q)"), start=True, stop=True)
+            nc.scalar.activation(out=rinv[:].rearrange("p n q -> p (n q)"), in_=rb[:], func=ACT.Abs_reciprocal_sqrt)
+            for n in range(B):
+                nc.vector.scalar_tensor_tensor(
+                    out=O[:, n, :].rearrange("p (i q) -> p i q", i=NI),
+                    in0=rinv[:, n, 0:T - 1].unsqueeze(1).to_broadcast([P, NI, T - 1]),
+                    scalar=1e12, in1=Tn[:, :, n, 0:T - 1], op0=ALU.min, op1=ALU.mult)
+                nc.sync.dma_start(out=out[n].rearrange("(m i) q -> m (i q)", i=NI), in_=O[:, n, :])
+
+        quant_x(0, 0, 4)
+        quant_x(1, 0, 4)
+        transposes(0, 2, "SS")
+        quant_x(0, 4, 2)
+        quant_x(1, 4, 2)
+        quantise(0, 2)
+        quant_x(0, 6, 1)
+        quant_x(1, 6, 1)
+        for K in WIDTHS:
+            nc.vector.tensor_copy(out=bias[:, K - 2, :], in_=braw[K][:])
+        transposes(0, 3, "SVS")
+        quantise(0, 3)
+        products(0, 2)
+        relu(0, 2)
+        transposes(0, 4, COPY_ENG[4])
+        quantise(0, 4)
+        products(0, 3)
+        relu(0, 3)
+        maxi(0, 3)
+        transposes(1, 2, COPY_ENG[2])
+        quantise(1, 2)
+        products(0, 4)
+        for i in range(1, NI):
+            if i + 2 < NI:
+                load(i + 2)
+            relu(i - 1, 4)
+            transposes(i, 3, COPY_ENG[3])
+            quantise(i, 3)
+            maxi(i - 1, 4)
+            transposes(i, 4, COPY_ENG[4])
+            quantise(i, 4)
+            if i + 1 < NI:
+                transposes(i + 1, 2, COPY_ENG[2])
+            square(i - 1)
+            if i + 1 < NI:
+                quantise(i + 1, 2)
+            addsq(i - 1)
+            products(i, 2)
+            relu(i, 2)
+            products(i, 3)
+            relu(i, 3)
+            maxi(i, 3)
+            products(i, 4)
+        relu(NI - 1, 4)
+        maxi(NI - 1, 4)
+        square(NI - 1)
+        addsq(NI - 1)
+        finish()

@@ -22,6 +22,7 @@ R = 4
 NPL = R + 3
 FLOPS = 2 * B * (127 * 2 + 126 * 3 + 125 * 4) * D * F
 MANUAL = True
+LAST = 2
 COPY_ENG = {2: "SS", 3: "VSV", 4: "SSVS"}
 
 
@@ -134,53 +135,98 @@ def tile_textheading_pa_kernel(tc, words_emb, W2, b2, W3, b3, W4, b4, out):
         tmp = {}
         sqs = {}
 
-        def products(i, K):
-            acc = accp.tile([P, 512], F32, name="acc%d" % K, tag="acc%d" % K)
-            accs[(i, K)] = acc
+        main = {"n0": 0, "nt": B, "xc": xc, "xs": xs}
+        halves = []
+
+        def make_half(h):
+            hc = NPL * 64
+            xgh = const.tile([P, 2 * hc * 4], BF16, name="xgh%d" % h, align_bytes=64)
+            xch = const.tile([P, 2, hc], U32, name="xch%d" % h, align_bytes=64)
+            xsh = const.tile([P, 2, hc], U8, name="xsh%d" % h, align_bytes=64)
+            nc.vector.tensor_copy(
+                out=xgh[:].bitcast(F32).rearrange("p (g r w) -> p g r w", g=2, r=NPL),
+                in_=xg_w[:, :, :, 2 * h:2 * h + 2, :, :].rearrange("p g r n q u -> p g r (n q u)"))
+            cf = xch[:].rearrange("p g c -> p (g c)")
+            sf = xsh[:].rearrange("p g c -> p (g c)")
+            for (a, w) in ((0, 2048), (2048, 1024), (3072, 512)):
+                nc.vector.quantize_mx(out=cf[:, a // 4:(a + w) // 4].bitcast(FP8X4),
+                                      scales=sf[:, a // 4:(a + w) // 4], in_=xgh[:, a:a + w])
+            halves.append({"n0": 2 * h, "nt": 2, "xc": xch, "xs": xsh})
+
+        def products(i, K, lay):
+            nt = lay["nt"]
+            n_cols = P * nt
+            pw = 32 * nt
+            acc = accp.tile([P, n_cols], F32, name="acc%d" % K, tag="acc%d" % K)
+            accs[(i, K, lay["n0"])] = acc
             cw, sc = cod[(i, K)]
             for k in range(K):
                 for g in range(2):
                     j = (2 * k + g) * P
                     nc.tensor.matmul_mx(out=acc[:], lhsT=cw[:, j:j + P].bitcast(FP8X4), lhsT_scale=sc[:, j:j + P],
-                                        rhs=xc[:, g, P * k:P * k + 512].bitcast(FP8X4),
-                                        rhs_scale=xs[:, g, P * k:P * k + 512],
+                                        rhs=lay["xc"][:, g, pw * k:pw * k + n_cols].bitcast(FP8X4),
+                                        rhs_scale=lay["xs"][:, g, pw * k:pw * k + n_cols],
                                         start=(k == 0 and g == 0), stop=(k == K - 1 and g == 1))
 
-        def relu(i, K):
+        def relu(i, K, lay):
+            n0 = lay["n0"]
+            nt = lay["nt"]
             if K == 2:
-                dst = Tn[:, i]
+                dst = Tn[:, i, n0:n0 + nt, :]
             else:
-                tmp[(i, K)] = epool.tile([P, B, T], F32, name="t%d" % K, tag="t%d" % K)
-                dst = tmp[(i, K)][:]
+                tmp[(i, K, n0)] = epool.tile([P, nt, T], F32, name="t%d" % K, tag="t%d" % K)
+                dst = tmp[(i, K, n0)][:]
             nc.scalar.activation(out=dst.rearrange("p n (q r) -> p n q r", r=R),
-                                 in_=accs[(i, K)][:].rearrange("p (r n q) -> p n q r", r=R, n=B),
+                                 in_=accs[(i, K, n0)][:].rearrange("p (r n q) -> p n q r", r=R, n=nt),
                                  func=ACT.Relu, bias=bias[:, K - 2, i:i + 1])
 
-        def maxi(i, K):
+        def maxi(i, K, lay):
+            n0 = lay["n0"]
+            nt = lay["nt"]
             v = T + 1 - K
-            nc.vector.tensor_tensor(out=Tn[:, i, :, 0:v], in0=Tn[:, i, :, 0:v], in1=tmp[(i, K)][:, :, 0:v], op=ALU.max)
+            nc.vector.tensor_tensor(out=Tn[:, i, n0:n0 + nt, 0:v], in0=Tn[:, i, n0:n0 + nt, 0:v],
+                                    in1=tmp[(i, K, n0)][:, :, 0:v], op=ALU.max)
 
-        def square(i):
+        def square(i, lay):
+            n0 = lay["n0"]
+            nt = lay["nt"]
             if i == 0:
                 nc.scalar.activation(out=ssum[:], in_=Tn[:, i], func=ACT.Square)
             else:
-                sqs[i] = epool.tile([P, B, T], F32, name="sq", tag="sq")
-                nc.scalar.activation(out=sqs[i][:], in_=Tn[:, i], func=ACT.Square)
+                sqs[(i, n0)] = epool.tile([P, nt, T], F32, name="sq", tag="sq")
+                nc.scalar.activation(out=sqs[(i, n0)][:], in_=Tn[:, i, n0:n0 + nt, :], func=ACT.Square)
 
-        def addsq(i):
+        def addsq(i, lay):
+            n0 = lay["n0"]
+            nt = lay["nt"]
             if i > 0:
-                nc.vector.tensor_tensor(out=ssum[:], in0=ssum[:], in1=sqs[i][:], op=ALU.add)
+                nc.vector.tensor_tensor(out=ssum[:, n0:n0 + nt, :], in0=ssum[:, n0:n0 + nt, :],
+                                        in1=sqs[(i, n0)][:], op=ALU.add)
 
-        def finish():
-            rb = tp.tile([P, 512], F32, name="rb", tag="tp")
-            nc.tensor.matmul(out=rb[:], lhsT=ones[:], rhs=ssum[:].rearrange("p n q -> p (n q)"), start=True, stop=True)
-            nc.scalar.activation(out=rinv[:].rearrange("p n q -> p (n q)"), in_=rb[:], func=ACT.Abs_reciprocal_sqrt)
-            for n in range(B):
-                nc.vector.scalar_tensor_tensor(
-                    out=O[:, n, :].rearrange("p (i q) -> p i q", i=NI),
-                    in0=rinv[:, n, 0:T - 1].unsqueeze(1).to_broadcast([P, NI, T - 1]),
-                    scalar=1e12, in1=Tn[:, :, n, 0:T - 1], op0=ALU.min, op1=ALU.mult)
-                nc.sync.dma_start(out=out[n].rearrange("(m i) q -> m (i q)", i=NI), in_=O[:, n, :])
+        rbs = {}
+
+        def norm_a(lay, whole):
+            n0 = lay["n0"]
+            nt = lay["nt"]
+            rbs[n0] = tp.tile([P, P * nt], F32, name="rb", tag="tp")
+            nc.tensor.matmul(out=rbs[n0][:], lhsT=ones[:], rhs=ssum[:, n0:n0 + nt, :].rearrange("p n q -> p (n q)"),
+                             start=True, stop=whole)
+
+        def norm_b(lay, whole):
+            n0 = lay["n0"]
+            nt = lay["nt"]
+            if not whole:
+                nc.tensor.matmul(out=rbs[n0][:], lhsT=ones[:], rhs=sqs[(NI - 1, n0)][:].rearrange("p n q -> p (n q)"),
+                                 start=False, stop=True)
+            nc.scalar.activation(out=rinv[:, n0:n0 + nt, :].rearrange("p n q -> p (n q)"), in_=rbs[n0][:],
+                                 func=ACT.Abs_reciprocal_sqrt)
+
+        def scale_store(n):
+            nc.vector.scalar_tensor_tensor(
+                out=O[:, n, :].rearrange("p (i q) -> p i q", i=NI),
+                in0=rinv[:, n, 0:T - 1].unsqueeze(1).to_broadcast([P, NI, T - 1]),
+                scalar=1e12, in1=Tn[:, :, n, 0:T - 1], op0=ALU.min, op1=ALU.mult)
+            nc.sync.dma_start(out=out[n].rearrange("(m i) q -> m (i q)", i=NI), in_=O[:, n, :])
 
         quant_x(0, 0, 4)
         quant_x(1, 0, 4)
@@ -194,39 +240,70 @@ def tile_textheading_pa_kernel(tc, words_emb, W2, b2, W3, b3, W4, b4, out):
             nc.vector.tensor_copy(out=bias[:, K - 2, :], in_=braw[K][:])
         transposes(0, 3, "SVS")
         quantise(0, 3)
-        products(0, 2)
-        relu(0, 2)
+        products(0, 2, main)
+        relu(0, 2, main)
         transposes(0, 4, COPY_ENG[4])
         quantise(0, 4)
-        products(0, 3)
-        relu(0, 3)
-        maxi(0, 3)
+        products(0, 3, main)
+        relu(0, 3, main)
+        maxi(0, 3, main)
         transposes(1, 2, COPY_ENG[2])
         quantise(1, 2)
-        products(0, 4)
+        products(0, 4, main)
+        def lay_of(i):
+            if i < NI - LAST:
+                return main
+            return halves[0]
+
         for i in range(1, NI):
             if i + 2 < NI:
                 load(i + 2)
-            relu(i - 1, 4)
+            relu(i - 1, 4, lay_of(i - 1))
             transposes(i, 3, COPY_ENG[3])
             quantise(i, 3)
-            maxi(i - 1, 4)
+            maxi(i - 1, 4, lay_of(i - 1))
             transposes(i, 4, COPY_ENG[4])
             quantise(i, 4)
             if i + 1 < NI:
                 transposes(i + 1, 2, COPY_ENG[2])
-            square(i - 1)
+            square(i - 1, lay_of(i - 1))
             if i + 1 < NI:
                 quantise(i + 1, 2)
-            addsq(i - 1)
-            products(i, 2)
-            relu(i, 2)
-            products(i, 3)
-            relu(i, 3)
-            maxi(i, 3)
-            products(i, 4)
-        relu(NI - 1, 4)
-        maxi(NI - 1, 4)
-        square(NI - 1)
-        addsq(NI - 1)
-        finish()
+            addsq(i - 1, lay_of(i - 1))
+            if i == 2 or i == 3:
+                make_half(i - 2)
+            products(i, 2, lay_of(i))
+            relu(i, 2, lay_of(i))
+            products(i, 3, lay_of(i))
+            relu(i, 3, lay_of(i))
+            maxi(i, 3, lay_of(i))
+            products(i, 4, lay_of(i))
+        hA = halves[0]
+        hB = halves[1]
+        last = NI - 1
+        relu(last, 4, hA)
+        for i in range(NI - LAST, NI):
+            products(i, 2, hB)
+            relu(i, 2, hB)
+            if i == NI - LAST:
+                maxi(last, 4, hA)
+                square(last, hA)
+                addsq(last, hA)
+            products(i, 3, hB)
+            relu(i, 3, hB)
+            maxi(i, 3, hB)
+            products(i, 4, hB)
+            relu(i, 4, hB)
+            maxi(i, 4, hB)
+            if i == NI - LAST:
+                norm_a(hA, True)
+                norm_b(hA, True)
+                scale_store(0)
+            square(i, hB)
+            if i < last:
+                addsq(i, hB)
+        norm_a(hB, False)
+        norm_b(hB, False)
+        scale_store(1)
+        scale_store(2)
+        scale_store(3)

@@ -20,10 +20,13 @@ NI = F // P
 WIDTHS = (2, 3, 4)
 R = 4
 NPL = R + 3
+HC = NPL * 64
 FLOPS = 2 * B * (127 * 2 + 126 * 3 + 125 * 4) * D * F
 MANUAL = True
 LAST = 2
-COPY_ENG = {2: "SS", 3: "VSV", 4: "SSVS"}
+FULL = (0, 4)
+HALF = ((0, 2), (2, 2))
+QCALLS = {2: ((0, 2048),), 3: ((0, 2048), (2048, 1024)), 4: ((0, 4096),)}
 
 
 def tile_textheading_pa_kernel(tc, words_emb, W2, b2, W3, b3, W4, b4, out):
@@ -45,7 +48,6 @@ def tile_textheading_pa_kernel(tc, words_emb, W2, b2, W3, b3, W4, b4, out):
         make_identity(nc, ident[:])
         ones = const.tile([P, P], F32, name="ones")
         nc.vector.memset(ones[:], 1.0)
-
         braw = {}
         for K in WIDTHS:
             braw[K] = const.tile([P, NI], BF16, name="braw%d" % K)
@@ -55,20 +57,28 @@ def tile_textheading_pa_kernel(tc, words_emb, W2, b2, W3, b3, W4, b4, out):
         nc.scalar.activation(out=warm[:], in_=ones[:, 0:1], func=ACT.Abs_reciprocal_sqrt)
 
         x_sb = const.tile([P, B, D], BF16, name="x_sb")
-        for n in range(B):
-            nc.sync.dma_start(out=x_sb[:, n, :], in_=words_emb[n])
         Wv = {}
         for K in WIDTHS:
             Wv[K] = Wd[K].rearrange("(m i) k d -> i m (k d)", i=NI)
         wraw = {}
 
-        def load(i):
-            for K in WIDTHS:
-                wraw[(i, K)] = wpool.tile([P, K * D], BF16, name="w%d" % K, tag="w%d" % K)
-                nc.sync.dma_start(out=wraw[(i, K)][:], in_=Wv[K][i])
+        def load_x(n):
+            nc.sync.dma_start(out=x_sb[:, n, :], in_=words_emb[n])
 
-        for i in range(3):
-            load(i)
+        def load_w(i, K):
+            wraw[(i, K)] = wpool.tile([P, K * D], BF16, name="w%d" % K, tag="w%d" % K)
+            nc.sync.dma_start(out=wraw[(i, K)][:], in_=Wv[K][i])
+
+        load_x(0)
+        load_x(1)
+        load_w(0, 2)
+        load_x(2)
+        load_x(3)
+        load_w(0, 3)
+        load_w(0, 4)
+        for i in (1, 2):
+            for K in WIDTHS:
+                load_w(i, K)
 
         def copy(eng, dst, src):
             if eng == "V":
@@ -76,14 +86,19 @@ def tile_textheading_pa_kernel(tc, words_emb, W2, b2, W3, b3, W4, b4, out):
             else:
                 nc.scalar.copy(out=dst, in_=src)
 
-        XC = NPL * B * 32
-        xg = const.tile([P, 2 * XC * 4], BF16, name="xg", align_bytes=64)
-        xg_w = xg[:].bitcast(F32).rearrange("p (g r n q u) -> p g r n q u", g=2, r=NPL, n=B, q=32, u=2)
-        xc = const.tile([P, 2, XC], U32, name="xc", align_bytes=64)
-        xs = const.tile([P, 2, XC], U8, name="xs", align_bytes=64)
-        for g in range(2):
-            nc.vector.memset(xg_w[:, g, R:NPL, :, 31:32, :], 0.0)
-        for n in range(B):
+        xgh = []
+        xgw = []
+        xch = []
+        xsh = []
+        for h in range(2):
+            xgh.append(const.tile([P, 2 * HC * 4], BF16, name="xgh%d" % h, align_bytes=64))
+            xgw.append(xgh[h][:].bitcast(F32).rearrange("p (g r n q u) -> p g r n q u", g=2, r=NPL, n=2, q=32, u=2))
+            xch.append(const.tile([P, 2, HC], U32, name="xch%d" % h, align_bytes=64))
+            xsh.append(const.tile([P, 2, HC], U8, name="xsh%d" % h, align_bytes=64))
+            for g in range(2):
+                nc.vector.memset(xgw[h][:, g, R:NPL, :, 31:32, :], 0.0)
+
+        def tx(n, eng):
             xb = tp.tile([P, 2, 2, P], F32, name="xb", tag="tp")
             xw = x_sb[:, n, :].bitcast(F32)
             for g in range(2):
@@ -91,16 +106,19 @@ def tile_textheading_pa_kernel(tc, words_emb, W2, b2, W3, b3, W4, b4, out):
                     o = 256 * g + 128 * u
                     nc.tensor.transpose(xb[:, g, u, :], xw[:, o:o + P], ident[:])
             for g in range(2):
-                copy("VS"[n % 2], xg_w[:, g, 0:R, n, :, :], xb[:, g, :, :].rearrange("p u (q r) -> p r q u", r=R))
-        for g in range(2):
-            nc.vector.tensor_copy(out=xg_w[:, g, R:NPL, :, 0:31, :], in_=xg_w[:, g, 0:3, :, 1:32, :])
+                copy(eng, xgw[n // 2][:, g, 0:R, n % 2, :, :], xb[:, g, :, :].rearrange("p u (q r) -> p r q u", r=R))
 
-        def quant_x(g, pl0, npl):
-            c0 = pl0 * P
-            w = npl * P
-            a = (g * XC + c0) * 4
-            nc.vector.quantize_mx(out=xc[:, g, c0:c0 + w].bitcast(FP8X4), scales=xs[:, g, c0:c0 + w],
-                                  in_=xg[:, a:a + 4 * w])
+        def shift(h):
+            for g in range(2):
+                nc.vector.tensor_copy(out=xgw[h][:, g, R:NPL, :, 0:31, :], in_=xgw[h][:, g, 0:3, :, 1:32, :])
+
+        def quant_h(h, pl0, npl):
+            c0 = pl0 * 64
+            w = npl * 64
+            for g in range(2):
+                a = (g * HC + c0) * 4
+                nc.vector.quantize_mx(out=xch[h][:, g, c0:c0 + w].bitcast(FP8X4), scales=xsh[h][:, g, c0:c0 + w],
+                                      in_=xgh[h][:, a:a + 4 * w])
 
         grp = {}
         cod = {}
@@ -123,7 +141,7 @@ def tile_textheading_pa_kernel(tc, words_emb, W2, b2, W3, b3, W4, b4, out):
             sc = cpool.tile([P, K * 256], U8, name="s%d" % K, tag="s%d" % K, align_bytes=64)
             cod[(i, K)] = (cw, sc)
             gr = grp[(i, K)]
-            for (a, w) in {2: ((0, 2048),), 3: ((0, 2048), (2048, 1024)), 4: ((0, 4096),)}[K]:
+            for (a, w) in QCALLS[K]:
                 nc.vector.quantize_mx(out=cw[:, a // 4:(a + w) // 4].bitcast(FP8X4),
                                       scales=sc[:, a // 4:(a + w) // 4], in_=gr[:, a:a + w])
 
@@ -132,92 +150,85 @@ def tile_textheading_pa_kernel(tc, words_emb, W2, b2, W3, b3, W4, b4, out):
         rinv = const.tile([P, B, T], F32, name="rinv")
         O = const.tile([P, B, NI * (T - 1)], F32, name="O")
         accs = {}
-        tmp = {}
+        tmps = {}
         sqs = {}
+        rbs = {}
 
-        main = {"n0": 0, "nt": B, "xc": xc, "xs": xs}
-        halves = []
+        def paired(i):
+            return i < NI - LAST
 
-        def make_half(h):
-            hc = NPL * 64
-            xgh = const.tile([P, 2 * hc * 4], BF16, name="xgh%d" % h, align_bytes=64)
-            xch = const.tile([P, 2, hc], U32, name="xch%d" % h, align_bytes=64)
-            xsh = const.tile([P, 2, hc], U8, name="xsh%d" % h, align_bytes=64)
-            nc.vector.tensor_copy(
-                out=xgh[:].bitcast(F32).rearrange("p (g r w) -> p g r w", g=2, r=NPL),
-                in_=xg_w[:, :, :, 2 * h:2 * h + 2, :, :].rearrange("p g r n q u -> p g r (n q u)"))
-            cf = xch[:].rearrange("p g c -> p (g c)")
-            sf = xsh[:].rearrange("p g c -> p (g c)")
-            for (a, w) in ((0, 2048), (2048, 1024), (3072, 512)):
-                nc.vector.quantize_mx(out=cf[:, a // 4:(a + w) // 4].bitcast(FP8X4),
-                                      scales=sf[:, a // 4:(a + w) // 4], in_=xgh[:, a:a + w])
-            halves.append({"n0": 2 * h, "nt": 2, "xc": xch, "xs": xsh})
-
-        def products(i, K, lay):
-            nt = lay["nt"]
-            n_cols = P * nt
-            pw = 32 * nt
-            acc = accp.tile([P, n_cols], F32, name="acc%d" % K, tag="acc%d" % K)
-            accs[(i, K, lay["n0"])] = acc
+        def products(i, K, h):
+            if paired(i):
+                if h == 0:
+                    acc = accp.tile([P, 512], F32, name="acc%d" % K, tag="acc%d" % K)
+                    accs[(i, K, 0)] = acc[:, 0:256]
+                    accs[(i, K, 1)] = acc[:, 256:512]
+            else:
+                acch = accp.tile([P, 256], F32, name="acc%d" % K, tag="acc%d" % K)
+                accs[(i, K, h)] = acch[:]
             cw, sc = cod[(i, K)]
             for k in range(K):
                 for g in range(2):
                     j = (2 * k + g) * P
-                    nc.tensor.matmul_mx(out=acc[:], lhsT=cw[:, j:j + P].bitcast(FP8X4), lhsT_scale=sc[:, j:j + P],
-                                        rhs=lay["xc"][:, g, pw * k:pw * k + n_cols].bitcast(FP8X4),
-                                        rhs_scale=lay["xs"][:, g, pw * k:pw * k + n_cols],
+                    nc.tensor.matmul_mx(out=accs[(i, K, h)], lhsT=cw[:, j:j + P].bitcast(FP8X4),
+                                        lhsT_scale=sc[:, j:j + P],
+                                        rhs=xch[h][:, g, 64 * k:64 * k + 256].bitcast(FP8X4),
+                                        rhs_scale=xsh[h][:, g, 64 * k:64 * k + 256],
                                         start=(k == 0 and g == 0), stop=(k == K - 1 and g == 1))
 
-        def relu(i, K, lay):
-            n0 = lay["n0"]
-            nt = lay["nt"]
+        def relu(i, K, h):
             if K == 2:
-                dst = Tn[:, i, n0:n0 + nt, :]
+                dst = Tn[:, i, 2 * h:2 * h + 2, :]
+            elif paired(i):
+                if h == 0:
+                    tf = epool.tile([P, B, T], F32, name="t%d" % K, tag="t%d" % K)
+                    tmps[(i, K, 0, 4)] = tf[:]
+                    tmps[(i, K, 0, 2)] = tf[:, 0:2, :]
+                    tmps[(i, K, 2, 2)] = tf[:, 2:4, :]
+                dst = tmps[(i, K, 2 * h, 2)]
             else:
-                tmp[(i, K, n0)] = epool.tile([P, nt, T], F32, name="t%d" % K, tag="t%d" % K)
-                dst = tmp[(i, K, n0)][:]
+                th = epool.tile([P, 2, T], F32, name="t%d" % K, tag="t%d" % K)
+                tmps[(i, K, 2 * h, 2)] = th[:]
+                dst = th[:]
             nc.scalar.activation(out=dst.rearrange("p n (q r) -> p n q r", r=R),
-                                 in_=accs[(i, K, n0)][:].rearrange("p (r n q) -> p n q r", r=R, n=nt),
+                                 in_=accs[(i, K, h)].rearrange("p (r n q) -> p n q r", r=R, n=2),
                                  func=ACT.Relu, bias=bias[:, K - 2, i:i + 1])
 
         def maxi(i, K, lay):
-            n0 = lay["n0"]
-            nt = lay["nt"]
+            n0, nt = lay
             v = T + 1 - K
             nc.vector.tensor_tensor(out=Tn[:, i, n0:n0 + nt, 0:v], in0=Tn[:, i, n0:n0 + nt, 0:v],
-                                    in1=tmp[(i, K, n0)][:, :, 0:v], op=ALU.max)
+                                    in1=tmps[(i, K, n0, nt)][:, :, 0:v], op=ALU.max)
 
         def square(i, lay):
-            n0 = lay["n0"]
-            nt = lay["nt"]
+            n0, nt = lay
             if i == 0:
                 nc.scalar.activation(out=ssum[:], in_=Tn[:, i], func=ACT.Square)
             else:
-                sqs[(i, n0)] = epool.tile([P, nt, T], F32, name="sq", tag="sq")
-                nc.scalar.activation(out=sqs[(i, n0)][:], in_=Tn[:, i, n0:n0 + nt, :], func=ACT.Square)
+                sq = epool.tile([P, nt, T], F32, name="sq", tag="sq")
+                sqs[(i, n0)] = sq
+                nc.scalar.activation(out=sq[:], in_=Tn[:, i, n0:n0 + nt, :], func=ACT.Square)
 
         def addsq(i, lay):
-            n0 = lay["n0"]
-            nt = lay["nt"]
+            n0, nt = lay
             if i > 0:
                 nc.vector.tensor_tensor(out=ssum[:, n0:n0 + nt, :], in0=ssum[:, n0:n0 + nt, :],
                                         in1=sqs[(i, n0)][:], op=ALU.add)
 
-        rbs = {}
-
-        def norm_a(lay, whole):
-            n0 = lay["n0"]
-            nt = lay["nt"]
-            rbs[n0] = tp.tile([P, P * nt], F32, name="rb", tag="tp")
-            nc.tensor.matmul(out=rbs[n0][:], lhsT=ones[:], rhs=ssum[:, n0:n0 + nt, :].rearrange("p n q -> p (n q)"),
+        def norm_sum(lay, whole):
+            n0, nt = lay
+            rb = tp.tile([P, P * nt], F32, name="rb", tag="tp")
+            rbs[n0] = rb
+            nc.tensor.matmul(out=rb[:], lhsT=ones[:], rhs=ssum[:, n0:n0 + nt, :].rearrange("p n q -> p (n q)"),
                              start=True, stop=whole)
 
-        def norm_b(lay, whole):
-            n0 = lay["n0"]
-            nt = lay["nt"]
-            if not whole:
-                nc.tensor.matmul(out=rbs[n0][:], lhsT=ones[:], rhs=sqs[(NI - 1, n0)][:].rearrange("p n q -> p (n q)"),
-                                 start=False, stop=True)
+        def norm_last(lay):
+            n0, nt = lay
+            nc.tensor.matmul(out=rbs[n0][:], lhsT=ones[:], rhs=sqs[(NI - 1, n0)][:].rearrange("p n q -> p (n q)"),
+                             start=False, stop=True)
+
+        def rsqrt(lay):
+            n0, nt = lay
             nc.scalar.activation(out=rinv[:, n0:n0 + nt, :].rearrange("p n q -> p (n q)"), in_=rbs[n0][:],
                                  func=ACT.Abs_reciprocal_sqrt)
 
@@ -228,82 +239,111 @@ def tile_textheading_pa_kernel(tc, words_emb, W2, b2, W3, b3, W4, b4, out):
                 scalar=1e12, in1=Tn[:, :, n, 0:T - 1], op0=ALU.min, op1=ALU.mult)
             nc.sync.dma_start(out=out[n].rearrange("(m i) q -> m (i q)", i=NI), in_=O[:, n, :])
 
-        quant_x(0, 0, 4)
-        quant_x(1, 0, 4)
+        def lay_of(i):
+            if paired(i):
+                return FULL
+            return HALF[0]
+
+        def halves_of(i):
+            if paired(i):
+                return (0, 1)
+            return (0,)
+
+        def prod_now(i, K):
+            for h in halves_of(i):
+                products(i, K, h)
+
+        def relu_now(i, K):
+            for h in halves_of(i):
+                relu(i, K, h)
+
+        tx(0, "V")
+        tx(1, "S")
+        quant_h(0, 0, 4)
         transposes(0, 2, "SS")
-        quant_x(0, 4, 2)
-        quant_x(1, 4, 2)
+        shift(0)
+        quant_h(0, 4, 2)
         quantise(0, 2)
-        quant_x(0, 6, 1)
-        quant_x(1, 6, 1)
+        quant_h(0, 6, 1)
+        tx(2, "V")
+        tx(3, "S")
+        products(0, 2, 0)
+        quant_h(1, 0, 4)
+        shift(1)
+        quant_h(1, 4, 2)
+        quant_h(1, 6, 1)
         for K in WIDTHS:
             nc.vector.tensor_copy(out=bias[:, K - 2, :], in_=braw[K][:])
         transposes(0, 3, "SVS")
         quantise(0, 3)
-        products(0, 2, main)
-        relu(0, 2, main)
-        transposes(0, 4, COPY_ENG[4])
+        products(0, 2, 1)
+        relu_now(0, 2)
+        transposes(0, 4, "VSVS")
         quantise(0, 4)
-        products(0, 3, main)
-        relu(0, 3, main)
-        maxi(0, 3, main)
-        transposes(1, 2, COPY_ENG[2])
+        prod_now(0, 3)
+        relu_now(0, 3)
+        maxi(0, 3, FULL)
+        transposes(1, 2, "SS")
         quantise(1, 2)
-        products(0, 4, main)
-        def lay_of(i):
-            if i < NI - LAST:
-                return main
-            return halves[0]
-
+        transposes(1, 3, "SVS")
+        quantise(1, 3)
+        prod_now(0, 4)
+        last = NI - 1
         for i in range(1, NI):
             if i + 2 < NI:
-                load(i + 2)
-            relu(i - 1, 4, lay_of(i - 1))
-            transposes(i, 3, COPY_ENG[3])
-            quantise(i, 3)
+                for K in WIDTHS:
+                    load_w(i + 2, K)
+            if i < last:
+                transposes(i, 4, "VSVS")
+            relu_now(i - 1, 4)
+            if i < last:
+                quantise(i, 4)
+                transposes(i + 1, 2, "VS")
+                transposes(i + 1, 3, "VSS")
             maxi(i - 1, 4, lay_of(i - 1))
-            transposes(i, 4, COPY_ENG[4])
-            quantise(i, 4)
-            if i + 1 < NI:
-                transposes(i + 1, 2, COPY_ENG[2])
-            square(i - 1, lay_of(i - 1))
-            if i + 1 < NI:
+            if i < last:
                 quantise(i + 1, 2)
+                quantise(i + 1, 3)
+            if i == last - 1:
+                transposes(last, 4, "VSVS")
+                quantise(last, 4)
+            prod_now(i, 2)
+            relu_now(i, 2)
+            square(i - 1, lay_of(i - 1))
             addsq(i - 1, lay_of(i - 1))
-            if i == 2 or i == 3:
-                make_half(i - 2)
-            products(i, 2, lay_of(i))
-            relu(i, 2, lay_of(i))
-            products(i, 3, lay_of(i))
-            relu(i, 3, lay_of(i))
+            prod_now(i, 3)
+            relu_now(i, 3)
             maxi(i, 3, lay_of(i))
-            products(i, 4, lay_of(i))
-        hA = halves[0]
-        hB = halves[1]
-        last = NI - 1
-        relu(last, 4, hA)
+            prod_now(i, 4)
+        hA = HALF[0]
+        hB = HALF[1]
+        relu(last, 4, 0)
         for i in range(NI - LAST, NI):
-            products(i, 2, hB)
-            relu(i, 2, hB)
+            products(i, 2, 1)
+            relu(i, 2, 1)
             if i == NI - LAST:
                 maxi(last, 4, hA)
                 square(last, hA)
                 addsq(last, hA)
-            products(i, 3, hB)
-            relu(i, 3, hB)
+            products(i, 3, 1)
+            relu(i, 3, 1)
             maxi(i, 3, hB)
-            products(i, 4, hB)
-            relu(i, 4, hB)
-            maxi(i, 4, hB)
+            products(i, 4, 1)
             if i == NI - LAST:
-                norm_a(hA, True)
-                norm_b(hA, True)
-                scale_store(0)
-            square(i, hB)
+                norm_sum(hA, True)
+            relu(i, 4, 1)
+            if i == NI - LAST:
+                rsqrt(hA)
+            maxi(i, 4, hB)
             if i < last:
+                square(i, hB)
                 addsq(i, hB)
-        norm_a(hB, False)
-        norm_b(hB, False)
+            if i == NI - LAST:
+                scale_store(0)
+        norm_sum(hB, False)
+        square(last, hB)
+        norm_last(hB)
+        rsqrt(hB)
         scale_store(1)
         scale_store(2)
         scale_store(3)

@@ -298,15 +298,7 @@ def tile_textheading_pa_kernel(tc, words_emb, W2, b2, W3, b3, W4, b4, out):
             relu_now(i - 1, 4)
             if i < last:
                 quantise(i, 4)
-                transposes(i + 1, 2, "VS")
-                transposes(i + 1, 3, "VSS")
             maxi(i - 1, 4, lay_of(i - 1))
-            if i < last:
-                quantise(i + 1, 2)
-                quantise(i + 1, 3)
-            if i == last - 1:
-                transposes(last, 4, "VSVS")
-                quantise(last, 4)
             prod_now(i, 2)
             relu_now(i, 2)
             square(i - 1, lay_of(i - 1))
@@ -314,6 +306,14 @@ def tile_textheading_pa_kernel(tc, words_emb, W2, b2, W3, b3, W4, b4, out):
             prod_now(i, 3)
             relu_now(i, 3)
             maxi(i, 3, lay_of(i))
+            if i < last:
+                transposes(i + 1, 2, "VS")
+                transposes(i + 1, 3, "VSS")
+                quantise(i + 1, 2)
+                quantise(i + 1, 3)
+            if i == last - 1:
+                transposes(last, 4, "VSVS")
+                quantise(last, 4)
             prod_now(i, 4)
         hA = HALF[0]
         hB = HALF[1]

@@ -22,7 +22,7 @@ R = 4
 NPL = R + 3
 HC = NPL * 64
 FLOPS = 2 * B * (127 * 2 + 126 * 3 + 125 * 4) * D * F
-MANUAL = True
+MANUAL = False
 LAST = 2
 FULL = (0, 4)
 HALF = ((0, 2), (2, 2))
@@ -298,7 +298,15 @@ def tile_textheading_pa_kernel(tc, words_emb, W2, b2, W3, b3, W4, b4, out):
             relu_now(i - 1, 4)
             if i < last:
                 quantise(i, 4)
+                transposes(i + 1, 2, "VS")
+                transposes(i + 1, 3, "VSS")
             maxi(i - 1, 4, lay_of(i - 1))
+            if i < last:
+                quantise(i + 1, 2)
+                quantise(i + 1, 3)
+            if i == last - 1:
+                transposes(last, 4, "VSVS")
+                quantise(last, 4)
             prod_now(i, 2)
             relu_now(i, 2)
             square(i - 1, lay_of(i - 1))
@@ -306,14 +314,6 @@ def tile_textheading_pa_kernel(tc, words_emb, W2, b2, W3, b3, W4, b4, out):
             prod_now(i, 3)
             relu_now(i, 3)
             maxi(i, 3, lay_of(i))
-            if i < last:
-                transposes(i + 1, 2, "VS")
-                transposes(i + 1, 3, "VSS")
-                quantise(i + 1, 2)
-                quantise(i + 1, 3)
-            if i == last - 1:
-                transposes(last, 4, "VSVS")
-                quantise(last, 4)
             prod_now(i, 4)
         hA = HALF[0]
         hB = HALF[1]

@@ -22,7 +22,7 @@ R = 4
 NPL = R + 3
 HC = NPL * 64
 FLOPS = 2 * B * (127 * 2 + 126 * 3 + 125 * 4) * D * F
-MANUAL = False
+MANUAL = True
 LAST = 2
 FULL = (0, 4)
 HALF = ((0, 2), (2, 2))
@@ -120,6 +120,25 @@ def tile_textheading_pa_kernel(tc, words_emb, W2, b2, W3, b3, W4, b4, out):
                 nc.vector.quantize_mx(out=xch[h][:, g, c0:c0 + w].bitcast(FP8X4), scales=xsh[h][:, g, c0:c0 + w],
                                       in_=xgh[h][:, a:a + 4 * w])
 
+        SC = 5 * 64
+        xc1 = {}
+        xs1 = {}
+
+        def make_single(t):
+            xg1 = const.tile([P, 2 * SC * 4], BF16, name="xg1_%d" % t, align_bytes=64)
+            xc1[t] = const.tile([P, 2, SC], U32, name="xc1_%d" % t, align_bytes=64)
+            xs1[t] = const.tile([P, 2, SC], U8, name="xs1_%d" % t, align_bytes=64)
+            xw1 = xg1[:].bitcast(F32).rearrange("p (g r q s u) -> p g r q s u", g=2, r=5, q=32, s=2, u=2)
+            for g in range(2):
+                for r in range(5):
+                    copy("VS"[(g * 5 + r) % 2], xw1[:, g, r],
+                         xgw[t // 2][:, g, r:r + 3:2, t % 2, :, :].rearrange("p s q u -> p q s u"))
+            cf = xc1[t][:].rearrange("p g c -> p (g c)")
+            sf = xs1[t][:].rearrange("p g c -> p (g c)")
+            for (a, w) in ((0, 2048), (2048, 512)):
+                nc.vector.quantize_mx(out=cf[:, a // 4:(a + w) // 4].bitcast(FP8X4),
+                                      scales=sf[:, a // 4:(a + w) // 4], in_=xg1[:, a:a + w])
+
         grp = {}
         cod = {}
 
@@ -192,6 +211,29 @@ def tile_textheading_pa_kernel(tc, words_emb, W2, b2, W3, b3, W4, b4, out):
                 dst = th[:]
             nc.scalar.activation(out=dst.rearrange("p n (q r) -> p n q r", r=R),
                                  in_=accs[(i, K, h)].rearrange("p (r n q) -> p n q r", r=R, n=2),
+                                 func=ACT.Relu, bias=bias[:, K - 2, i:i + 1])
+
+        def products1(i, K, t):
+            acc1 = accp.tile([P, P], F32, name="acc%d" % K, tag="acc%d" % K)
+            accs[(i, K, t + 10)] = acc1[:]
+            cw, sc = cod[(i, K)]
+            for k in range(K):
+                for g in range(2):
+                    j = (2 * k + g) * P
+                    nc.tensor.matmul_mx(out=acc1[:], lhsT=cw[:, j:j + P].bitcast(FP8X4), lhsT_scale=sc[:, j:j + P],
+                                        rhs=xc1[t][:, g, 64 * k:64 * k + P].bitcast(FP8X4),
+                                        rhs_scale=xs1[t][:, g, 64 * k:64 * k + P],
+                                        start=(k == 0 and g == 0), stop=(k == K - 1 and g == 1))
+
+        def relu1(i, K, t):
+            if K == 2:
+                dst = Tn[:, i, t, :]
+            else:
+                t1 = epool.tile([P, 1, T], F32, name="t%d" % K, tag="t%d" % K)
+                tmps[(i, K, t, 1)] = t1[:]
+                dst = t1[:, 0, :]
+            nc.scalar.activation(out=dst.rearrange("p (q r) -> p q r", r=2),
+                                 in_=accs[(i, K, t + 10)].rearrange("p (r q) -> p q r", r=2),
                                  func=ACT.Relu, bias=bias[:, K - 2, i:i + 1])
 
         def maxi(i, K, lay):
@@ -311,39 +353,58 @@ def tile_textheading_pa_kernel(tc, words_emb, W2, b2, W3, b3, W4, b4, out):
             relu_now(i, 2)
             square(i - 1, lay_of(i - 1))
             addsq(i - 1, lay_of(i - 1))
+            if i == 2 or i == 3:
+                make_single(i)
             prod_now(i, 3)
             relu_now(i, 3)
             maxi(i, 3, lay_of(i))
             prod_now(i, 4)
         hA = HALF[0]
         hB = HALF[1]
+        tC = (2, 1)
+        tD = (3, 1)
+        prev = last - 1
         relu(last, 4, 0)
-        for i in range(NI - LAST, NI):
-            products(i, 2, 1)
-            relu(i, 2, 1)
-            if i == NI - LAST:
-                maxi(last, 4, hA)
-                square(last, hA)
-                addsq(last, hA)
-            products(i, 3, 1)
-            relu(i, 3, 1)
-            maxi(i, 3, hB)
-            products(i, 4, 1)
-            if i == NI - LAST:
-                norm_sum(hA, True)
-            relu(i, 4, 1)
-            if i == NI - LAST:
-                rsqrt(hA)
-            maxi(i, 4, hB)
-            if i < last:
-                square(i, hB)
-                addsq(i, hB)
-            if i == NI - LAST:
-                scale_store(0)
-        norm_sum(hB, False)
-        square(last, hB)
-        norm_last(hB)
-        rsqrt(hB)
+        products(prev, 2, 1)
+        relu(prev, 2, 1)
+        maxi(last, 4, hA)
+        square(last, hA)
+        addsq(last, hA)
+        products(prev, 3, 1)
+        relu(prev, 3, 1)
+        maxi(prev, 3, hB)
+        products(prev, 4, 1)
+        norm_sum(hA, True)
+        relu(prev, 4, 1)
+        rsqrt(hA)
+        maxi(prev, 4, hB)
+        square(prev, hB)
+        addsq(prev, hB)
+        scale_store(0)
+        products1(last, 2, 2)
+        relu1(last, 2, 2)
+        products1(last, 3, 2)
+        relu1(last, 3, 2)
+        maxi(last, 3, tC)
+        products1(last, 4, 2)
+        relu1(last, 4, 2)
+        maxi(last, 4, tC)
+        square(last, tC)
         scale_store(1)
+        products1(last, 2, 3)
+        relu1(last, 2, 3)
+        products1(last, 3, 3)
+        relu1(last, 3, 3)
+        maxi(last, 3, tD)
+        products1(last, 4, 3)
+        norm_sum(tC, False)
+        norm_last(tC)
+        norm_sum(tD, False)
+        relu1(last, 4, 3)
+        rsqrt(tC)
+        maxi(last, 4, tD)
+        square(last, tD)
+        norm_last(tD)
         scale_store(2)
+        rsqrt(tD)
         scale_store(3)

@@ -23,7 +23,8 @@ NPL = R + 3
 HC = NPL * 64
 FLOPS = 2 * B * (127 * 2 + 126 * 3 + 125 * 4) * D * F
 MANUAL = True
-LAST = 2
+LAST = 1
+ALT = "VSVSVSVS"
 FULL = (0, 4)
 HALF = ((0, 2), (2, 2))
 QCALLS = {2: ((0, 2048),), 3: ((0, 2048), (2048, 1024)), 4: ((0, 4096),)}
@@ -38,7 +39,7 @@ def tile_textheading_pa_kernel(tc, words_emb, W2, b2, W3, b3, W4, b4, out):
             ctx.enter_context(tc.manual_schedule())
         const = ctx.enter_context(tc.tile_pool(name="const", bufs=1))
         wpool = ctx.enter_context(tc.tile_pool(name="wraw", bufs=3))
-        gpool = ctx.enter_context(tc.tile_pool(name="grp", bufs=2))
+        gpool = ctx.enter_context(tc.tile_pool(name="grp", bufs=3))
         cpool = ctx.enter_context(tc.tile_pool(name="codes", bufs=3))
         epool = ctx.enter_context(tc.tile_pool(name="epi", bufs=2))
         tp = ctx.enter_context(tc.psum_pool(name="tp", bufs=5))
@@ -120,25 +121,6 @@ def tile_textheading_pa_kernel(tc, words_emb, W2, b2, W3, b3, W4, b4, out):
                 nc.vector.quantize_mx(out=xch[h][:, g, c0:c0 + w].bitcast(FP8X4), scales=xsh[h][:, g, c0:c0 + w],
                                       in_=xgh[h][:, a:a + 4 * w])
 
-        SC = 5 * 64
-        xc1 = {}
-        xs1 = {}
-
-        def make_single(t):
-            xg1 = const.tile([P, 2 * SC * 4], BF16, name="xg1_%d" % t, align_bytes=64)
-            xc1[t] = const.tile([P, 2, SC], U32, name="xc1_%d" % t, align_bytes=64)
-            xs1[t] = const.tile([P, 2, SC], U8, name="xs1_%d" % t, align_bytes=64)
-            xw1 = xg1[:].bitcast(F32).rearrange("p (g r q s u) -> p g r q s u", g=2, r=5, q=32, s=2, u=2)
-            for g in range(2):
-                for r in range(5):
-                    copy("VS"[(g * 5 + r) % 2], xw1[:, g, r],
-                         xgw[t // 2][:, g, r:r + 3:2, t % 2, :, :].rearrange("p s q u -> p q s u"))
-            cf = xc1[t][:].rearrange("p g c -> p (g c)")
-            sf = xs1[t][:].rearrange("p g c -> p (g c)")
-            for (a, w) in ((0, 2048), (2048, 512)):
-                nc.vector.quantize_mx(out=cf[:, a // 4:(a + w) // 4].bitcast(FP8X4),
-                                      scales=sf[:, a // 4:(a + w) // 4], in_=xg1[:, a:a + w])
-
         grp = {}
         cod = {}
 
@@ -154,6 +136,8 @@ def tile_textheading_pa_kernel(tc, words_emb, W2, b2, W3, b3, W4, b4, out):
                         o = 512 * k + 256 * g + 128 * u
                         nc.tensor.transpose(bank[:, g, u, :], ww[:, o:o + P], ident[:])
                 copy(engs[k], gr_w[:, k], bank[:].rearrange("p g u f -> p g f u"))
+            if i + 3 < NI:
+                load_w(i + 3, K)
 
         def quantise(i, K):
             cw = cpool.tile([P, K * 256], U32, name="c%d" % K, tag="c%d" % K, align_bytes=64)
@@ -211,29 +195,6 @@ def tile_textheading_pa_kernel(tc, words_emb, W2, b2, W3, b3, W4, b4, out):
                 dst = th[:]
             nc.scalar.activation(out=dst.rearrange("p n (q r) -> p n q r", r=R),
                                  in_=accs[(i, K, h)].rearrange("p (r n q) -> p n q r", r=R, n=2),
-                                 func=ACT.Relu, bias=bias[:, K - 2, i:i + 1])
-
-        def products1(i, K, t):
-            acc1 = accp.tile([P, P], F32, name="acc%d" % K, tag="acc%d" % K)
-            accs[(i, K, t + 10)] = acc1[:]
-            cw, sc = cod[(i, K)]
-            for k in range(K):
-                for g in range(2):
-                    j = (2 * k + g) * P
-                    nc.tensor.matmul_mx(out=acc1[:], lhsT=cw[:, j:j + P].bitcast(FP8X4), lhsT_scale=sc[:, j:j + P],
-                                        rhs=xc1[t][:, g, 64 * k:64 * k + P].bitcast(FP8X4),
-                                        rhs_scale=xs1[t][:, g, 64 * k:64 * k + P],
-                                        start=(k == 0 and g == 0), stop=(k == K - 1 and g == 1))
-
-        def relu1(i, K, t):
-            if K == 2:
-                dst = Tn[:, i, t, :]
-            else:
-                t1 = epool.tile([P, 1, T], F32, name="t%d" % K, tag="t%d" % K)
-                tmps[(i, K, t, 1)] = t1[:]
-                dst = t1[:, 0, :]
-            nc.scalar.activation(out=dst.rearrange("p (q r) -> p q r", r=2),
-                                 in_=accs[(i, K, t + 10)].rearrange("p (r q) -> p q r", r=2),
                                  func=ACT.Relu, bias=bias[:, K - 2, i:i + 1])
 
         def maxi(i, K, lay):
@@ -331,80 +292,62 @@ def tile_textheading_pa_kernel(tc, words_emb, W2, b2, W3, b3, W4, b4, out):
         quantise(1, 3)
         prod_now(0, 4)
         last = NI - 1
-        for i in range(1, NI):
-            if i + 2 < NI:
-                for K in WIDTHS:
-                    load_w(i + 2, K)
-            if i < last:
-                transposes(i, 4, "VSVS")
-            relu_now(i - 1, 4)
-            if i < last:
-                quantise(i, 4)
-                transposes(i + 1, 2, "VS")
-                transposes(i + 1, 3, "VSS")
-            maxi(i - 1, 4, lay_of(i - 1))
-            if i < last:
-                quantise(i + 1, 2)
-                quantise(i + 1, 3)
-            if i == last - 1:
-                transposes(last, 4, "VSVS")
-                quantise(last, 4)
-            prod_now(i, 2)
-            relu_now(i, 2)
-            square(i - 1, lay_of(i - 1))
-            addsq(i - 1, lay_of(i - 1))
-            if i == 2 or i == 3:
-                make_single(i)
-            prod_now(i, 3)
-            relu_now(i, 3)
-            maxi(i, 3, lay_of(i))
-            prod_now(i, 4)
+        prev = 0
+        for a in (1, 3, 5):
+            units = [(a, 4), (a + 1, 2), (a + 1, 3), (a + 1, 4), (a + 2, 2), (a + 2, 3)]
+            tiles = [a, a + 1]
+            if a + 2 == last:
+                units.append((last, 4))
+                tiles.append(last)
+            b = 0
+            for (i, K) in units:
+                transposes(i, K, ALT[b % 2:b % 2 + K])
+                b += K
+            relu_now(prev, 4)
+            quantise(a, 4)
+            maxi(prev, 4, lay_of(prev))
+            todo = units[1:]
+            for idx in range(len(tiles)):
+                i = tiles[idx]
+                prod_now(i, 2)
+                relu_now(i, 2)
+                if 3 * idx < len(todo):
+                    quantise(*todo[3 * idx])
+                square(prev, lay_of(prev))
+                if 3 * idx + 1 < len(todo):
+                    quantise(*todo[3 * idx + 1])
+                addsq(prev, lay_of(prev))
+                prod_now(i, 3)
+                relu_now(i, 3)
+                if 3 * idx + 2 < len(todo):
+                    quantise(*todo[3 * idx + 2])
+                maxi(i, 3, lay_of(i))
+                prod_now(i, 4)
+                if idx < len(tiles) - 1:
+                    relu_now(i, 4)
+                    maxi(i, 4, lay_of(i))
+                prev = i
         hA = HALF[0]
         hB = HALF[1]
-        tC = (2, 1)
-        tD = (3, 1)
-        prev = last - 1
         relu(last, 4, 0)
-        products(prev, 2, 1)
-        relu(prev, 2, 1)
+        products(last, 2, 1)
+        relu(last, 2, 1)
         maxi(last, 4, hA)
         square(last, hA)
         addsq(last, hA)
-        products(prev, 3, 1)
-        relu(prev, 3, 1)
-        maxi(prev, 3, hB)
-        products(prev, 4, 1)
+        products(last, 3, 1)
+        relu(last, 3, 1)
+        maxi(last, 3, hB)
+        products(last, 4, 1)
         norm_sum(hA, True)
-        relu(prev, 4, 1)
+        relu(last, 4, 1)
         rsqrt(hA)
-        maxi(prev, 4, hB)
-        square(prev, hB)
-        addsq(prev, hB)
+        maxi(last, 4, hB)
+        norm_sum(hB, False)
+        square(last, hB)
+        norm_last(hB)
         scale_store(0)
-        products1(last, 2, 2)
-        relu1(last, 2, 2)
-        products1(last, 3, 2)
-        relu1(last, 3, 2)
-        maxi(last, 3, tC)
-        products1(last, 4, 2)
-        relu1(last, 4, 2)
-        maxi(last, 4, tC)
-        square(last, tC)
+        rsqrt(hB)
         scale_store(1)
-        products1(last, 2, 3)
-        relu1(last, 2, 3)
-        products1(last, 3, 3)
-        relu1(last, 3, 3)
-        maxi(last, 3, tD)
-        products1(last, 4, 3)
-        norm_sum(tC, False)
-        norm_last(tC)
-        norm_sum(tD, False)
-        relu1(last, 4, 3)
-        rsqrt(tC)
-        maxi(last, 4, tD)
-        square(last, tD)
-        norm_last(tD)
         scale_store(2)
-        rsqrt(tD)
         scale_store(3)

from contextlib import ExitStack

import concourse.mybir as mybir
from concourse.masks import make_identity

F32 = mybir.dt.float32
BF16 = mybir.dt.bfloat16
U32 = mybir.dt.uint32
U8 = mybir.dt.uint8
FP8X4 = mybir.dt.float8_e4m3fn_x4
ACT = mybir.ActivationFunctionType
ALU = mybir.AluOpType

P = 128
B = 4
T = 128
D = 1024
F = 1024
NI = F // P
WIDTHS = (2, 3, 4)
R = 4
NPL = R + 3
HC = NPL * 64
FLOPS = 2 * B * (127 * 2 + 126 * 3 + 125 * 4) * D * F
MANUAL = True
LAST = 1
ALT = "VSVSVSVS"
FULL = (0, 4)
HALF = ((0, 2), (2, 2))
QCALLS = {2: ((0, 2048),), 3: ((0, 2048), (2048, 1024)), 4: ((0, 4096),)}


def tile_textheading_pa_kernel(tc, words_emb, W2, b2, W3, b3, W4, b4, out):
    nc = tc.nc
    Wd = {2: W2, 3: W3, 4: W4}
    bd = {2: b2, 3: b3, 4: b4}
    with ExitStack() as ctx:
        if MANUAL:
            ctx.enter_context(tc.manual_schedule())
        const = ctx.enter_context(tc.tile_pool(name="const", bufs=1))
        wpool = ctx.enter_context(tc.tile_pool(name="wraw", bufs=3))
        gpool = ctx.enter_context(tc.tile_pool(name="grp", bufs=3))
        cpool = ctx.enter_context(tc.tile_pool(name="codes", bufs=3))
        epool = ctx.enter_context(tc.tile_pool(name="epi", bufs=2))
        tp = ctx.enter_context(tc.psum_pool(name="tp", bufs=5))
        accp = ctx.enter_context(tc.psum_pool(name="acc", bufs=1))

        ident = const.tile([P, P], F32, name="ident")
        make_identity(nc, ident[:])
        ones = const.tile([P, P], F32, name="ones")
        nc.vector.memset(ones[:], 1.0)
        braw = {}
        for K in WIDTHS:
            braw[K] = const.tile([P, NI], BF16, name="braw%d" % K)
            nc.scalar.dma_start(out=braw[K][:], in_=bd[K].rearrange("(m i) -> m i", i=NI))
        bias = const.tile([P, 3, NI], F32, name="bias")
        warm = const.tile([P, 1], F32, name="warm")
        nc.scalar.activation(out=warm[:], in_=ones[:, 0:1], func=ACT.Abs_reciprocal_sqrt)

        x_sb = const.tile([P, B, D], BF16, name="x_sb")
        Wv = {}
        for K in WIDTHS:
            Wv[K] = Wd[K].rearrange("(m i) k d -> i m (k d)", i=NI)
        wraw = {}

        def load_x(n):
            nc.sync.dma_start(out=x_sb[:, n, :], in_=words_emb[n])

        def load_w(i, K):
            wraw[(i, K)] = wpool.tile([P, K * D], BF16, name="w%d" % K, tag="w%d" % K)
            nc.sync.dma_start(out=wraw[(i, K)][:], in_=Wv[K][i])

        load_x(0)
        load_x(1)
        load_w(0, 2)
        load_x(2)
        load_x(3)
        load_w(0, 3)
        load_w(0, 4)
        for i in (1, 2):
            for K in WIDTHS:
                load_w(i, K)

        def copy(eng, dst, src):
            if eng == "V":
                nc.vector.tensor_copy(out=dst, in_=src)
            else:
                nc.scalar.copy(out=dst, in_=src)

        xgh = []
        xgw = []
        xch = []
        xsh = []
        for h in range(2):
            xgh.append(const.tile([P, 2 * HC * 4], BF16, name="xgh%d" % h, align_bytes=64))
            xgw.append(xgh[h][:].bitcast(F32).rearrange("p (g r n q u) -> p g r n q u", g=2, r=NPL, n=2, q=32, u=2))
            xch.append(const.tile([P, 2, HC], U32, name="xch%d" % h, align_bytes=64))
            xsh.append(const.tile([P, 2, HC], U8, name="xsh%d" % h, align_bytes=64))
            for g in range(2):
                nc.vector.memset(xgw[h][:, g, R:NPL, :, 31:32, :], 0.0)

        def tx(n, eng):
            xb = tp.tile([P, 2, 2, P], F32, name="xb", tag="tp")
            xw = x_sb[:, n, :].bitcast(F32)
            for g in range(2):
                for u in range(2):
                    o = 256 * g + 128 * u
                    nc.tensor.transpose(xb[:, g, u, :], xw[:, o:o + P], ident[:])
            for g in range(2):
                copy(eng, xgw[n // 2][:, g, 0:R, n % 2, :, :], xb[:, g, :, :].rearrange("p u (q r) -> p r q u", r=R))

        def shift(h):
            for g in range(2):
                nc.vector.tensor_copy(out=xgw[h][:, g, R:NPL, :, 0:31, :], in_=xgw[h][:, g, 0:3, :, 1:32, :])

        def quant_h(h, pl0, npl):
            c0 = pl0 * 64
            w = npl * 64
            for g in range(2):
                a = (g * HC + c0) * 4
                nc.vector.quantize_mx(out=xch[h][:, g, c0:c0 + w].bitcast(FP8X4), scales=xsh[h][:, g, c0:c0 + w],
                                      in_=xgh[h][:, a:a + 4 * w])

        grp = {}
        cod = {}

        def transposes(i, K, engs):
            gr = gpool.tile([P, K * 1024], BF16, name="g%d" % K, tag="g%d" % K, align_bytes=64)
            grp[(i, K)] = gr
            gr_w = gr[:].bitcast(F32).rearrange("p (k g f u) -> p k g f u", k=K, g=2, f=P, u=2)
            ww = wraw[(i, K)][:].bitcast(F32)
            for k in range(K):
                bank = tp.tile([P, 2, 2, P], F32, name="bank", tag="tp")
                for g in range(2):
                    for u in range(2):
                        o = 512 * k + 256 * g + 128 * u
                        nc.tensor.transpose(bank[:, g, u, :], ww[:, o:o + P], ident[:])
                copy(engs[k], gr_w[:, k], bank[:].rearrange("p g u f -> p g f u"))
            if i + 3 < NI:
                load_w(i + 3, K)

        def quantise(i, K):
            cw = cpool.tile([P, K * 256], U32, name="c%d" % K, tag="c%d" % K, align_bytes=64)
            sc = cpool.tile([P, K * 256], U8, name="s%d" % K, tag="s%d" % K, align_bytes=64)
            cod[(i, K)] = (cw, sc)
            gr = grp[(i, K)]
            for (a, w) in QCALLS[K]:
                nc.vector.quantize_mx(out=cw[:, a // 4:(a + w) // 4].bitcast(FP8X4),
                                      scales=sc[:, a // 4:(a + w) // 4], in_=gr[:, a:a + w])

        Tn = const.tile([P, NI, B, T], F32, name="Tn")
        ssum = const.tile([P, B, T], F32, name="ssum")
        rinv = const.tile([P, B, T], F32, name="rinv")
        O = const.tile([P, B, NI * (T - 1)], F32, name="O")
        accs = {}
        tmps = {}
        sqs = {}
        rbs = {}

        def paired(i):
            return i < NI - LAST

        def products(i, K, h):
            if paired(i):
                if h == 0:
                    acc = accp.tile([P, 512], F32, name="acc%d" % K, tag="acc%d" % K)
                    accs[(i, K, 0)] = acc[:, 0:256]
                    accs[(i, K, 1)] = acc[:, 256:512]
            else:
                acch = accp.tile([P, 256], F32, name="acc%d" % K, tag="acc%d" % K)
                accs[(i, K, h)] = acch[:]
            cw, sc = cod[(i, K)]
            for k in range(K):
                for g in range(2):
                    j = (2 * k + g) * P
                    nc.tensor.matmul_mx(out=accs[(i, K, h)], lhsT=cw[:, j:j + P].bitcast(FP8X4),
                                        lhsT_scale=sc[:, j:j + P],
                                        rhs=xch[h][:, g, 64 * k:64 * k + 256].bitcast(FP8X4),
                                        rhs_scale=xsh[h][:, g, 64 * k:64 * k + 256],
                                        start=(k == 0 and g == 0), stop=(k == K - 1 and g == 1))

        def relu(i, K, h):
            if K == 2:
                dst = Tn[:, i, 2 * h:2 * h + 2, :]
            elif paired(i):
                if h == 0:
                    tf = epool.tile([P, B, T], F32, name="t%d" % K, tag="t%d" % K)
                    tmps[(i, K, 0, 4)] = tf[:]
                    tmps[(i, K, 0, 2)] = tf[:, 0:2, :]
                    tmps[(i, K, 2, 2)] = tf[:, 2:4, :]
                dst = tmps[(i, K, 2 * h, 2)]
            else:
                th = epool.tile([P, 2, T], F32, name="t%d" % K, tag="t%d" % K)
                tmps[(i, K, 2 * h, 2)] = th[:]
                dst = th[:]
            nc.scalar.activation(out=dst.rearrange("p n (q r) -> p n q r", r=R),
                                 in_=accs[(i, K, h)].rearrange("p (r n q) -> p n q r", r=R, n=2),
                                 func=ACT.Relu, bias=bias[:, K - 2, i:i + 1])

        def maxi(i, K, lay):
            n0, nt = lay
            v = T + 1 - K
            nc.vector.tensor_tensor(out=Tn[:, i, n0:n0 + nt, 0:v], in0=Tn[:, i, n0:n0 + nt, 0:v],
                                    in1=tmps[(i, K, n0, nt)][:, :, 0:v], op=ALU.max)

        def square(i, lay):
            n0, nt = lay
            if i == 0:
                nc.scalar.activation(out=ssum[:], in_=Tn[:, i], func=ACT.Square)
            else:
                sq = epool.tile([P, nt, T], F32, name="sq", tag="sq")
                sqs[(i, n0)] = sq
                nc.scalar.activation(out=sq[:], in_=Tn[:, i, n0:n0 + nt, :], func=ACT.Square)

        def addsq(i, lay):
            n0, nt = lay
            if i > 0:
                nc.vector.tensor_tensor(out=ssum[:, n0:n0 + nt, :], in0=ssum[:, n0:n0 + nt, :],
                                        in1=sqs[(i, n0)][:], op=ALU.add)

        def norm_sum(lay, whole):
            n0, nt = lay
            rb = tp.tile([P, P * nt], F32, name="rb", tag="tp")
            rbs[n0] = rb
            nc.tensor.matmul(out=rb[:], lhsT=ones[:], rhs=ssum[:, n0:n0 + nt, :].rearrange("p n q -> p (n q)"),
                             start=True, stop=whole)

        def norm_last(lay):
            n0, nt = lay
            nc.tensor.matmul(out=rbs[n0][:], lhsT=ones[:], rhs=sqs[(NI - 1, n0)][:].rearrange("p n q -> p (n q)"),
                             start=False, stop=True)

        def rsqrt(lay):
            n0, nt = lay
            nc.scalar.activation(out=rinv[:, n0:n0 + nt, :].rearrange("p n q -> p (n q)"), in_=rbs[n0][:],
                                 func=ACT.Abs_reciprocal_sqrt)

        def scale_store(n):
            nc.vector.scalar_tensor_tensor(
                out=O[:, n, :].rearrange("p (i q) -> p i q", i=NI),
                in0=rinv[:, n, 0:T - 1].unsqueeze(1).to_broadcast([P, NI, T - 1]),
                scalar=1e12, in1=Tn[:, :, n, 0:T - 1], op0=ALU.min, op1=ALU.mult)
            nc.sync.dma_start(out=out[n].rearrange("(m i) q -> m (i q)", i=NI), in_=O[:, n, :])

        def lay_of(i):
            if paired(i):
                return FULL
            return HALF[0]

        def halves_of(i):
            if paired(i):
                return (0, 1)
            return (0,)

        def prod_now(i, K):
            for h in halves_of(i):
                products(i, K, h)

        def relu_now(i, K):
            for h in halves_of(i):
                relu(i, K, h)

        tx(0, "V")
        tx(1, "S")
        quant_h(0, 0, 4)
        transposes(0, 2, "SS")
        shift(0)
        quant_h(0, 4, 2)
        quantise(0, 2)
        quant_h(0, 6, 1)
        tx(2, "V")
        tx(3, "S")
        products(0, 2, 0)
        quant_h(1, 0, 4)
        shift(1)
        quant_h(1, 4, 2)
        quant_h(1, 6, 1)
        for K in WIDTHS:
            nc.vector.tensor_copy(out=bias[:, K - 2, :], in_=braw[K][:])
        transposes(0, 3, "SVS")
        quantise(0, 3)
        products(0, 2, 1)
        relu_now(0, 2)
        transposes(0, 4, "VSVS")
        quantise(0, 4)
        prod_now(0, 3)
        relu_now(0, 3)
        maxi(0, 3, FULL)
        transposes(1, 2, "SS")
        quantise(1, 2)
        transposes(1, 3, "SVS")
        quantise(1, 3)
        prod_now(0, 4)
        last = NI - 1
        prev = 0
        for a in (1, 3, 5):
            units = [(a, 4), (a + 1, 2), (a + 1, 3), (a + 1, 4), (a + 2, 2), (a + 2, 3)]
            tiles = [a, a + 1]
            if a + 2 == last:
                units.append((last, 4))
                tiles.append(last)
            b = 0
            for (i, K) in units:
                transposes(i, K, ALT[b % 2:b % 2 + K])
                b += K
            relu_now(prev, 4)
            quantise(a, 4)
            maxi(prev, 4, lay_of(prev))
            todo = units[1:]
            for idx in range(len(tiles)):
                i = tiles[idx]
                prod_now(i, 2)
                relu_now(i, 2)
                if 3 * idx < len(todo):
                    quantise(*todo[3 * idx])
                square(prev, lay_of(prev))
                if 3 * idx + 1 < len(todo):
                    quantise(*todo[3 * idx + 1])
                addsq(prev, lay_of(prev))
                prod_now(i, 3)
                relu_now(i, 3)
                if 3 * idx + 2 < len(todo):
                    quantise(*todo[3 * idx + 2])
                maxi(i, 3, lay_of(i))
                prod_now(i, 4)
                if idx < len(tiles) - 1:
                    relu_now(i, 4)
                    maxi(i, 4, lay_of(i))
                prev = i
        hA = HALF[0]
        hB = HALF[1]
        relu(last, 4, 0)
        products(last, 2, 1)
        relu(last, 2, 1)
        maxi(last, 4, hA)
        square(last, hA)
        addsq(last, hA)
        products(last, 3, 1)
        relu(last, 3, 1)
        maxi(last, 3, hB)
        products(last, 4, 1)
        norm_sum(hA, True)
        relu(last, 4, 1)
        rsqrt(hA)
        maxi(last, 4, hB)
        norm_sum(hB, False)
        square(last, hB)
        norm_last(hB)
        scale_store(0)
        rsqrt(hB)
        scale_store(1)
        scale_store(2)
        scale_store(3)
